import numpy as np
import ml_dtypes


def mxq(x, axis, fmt="e4m3"):
    dtype, down = {"e4m3": (ml_dtypes.float8_e4m3fn, 7), "e5m2": (ml_dtypes.float8_e5m2, 14)}[fmt]
    v = np.moveaxis(np.asarray(x, np.float32).astype(ml_dtypes.bfloat16).astype(np.float64), axis, -1)
    blocks = v.reshape(v.shape[:-1] + (-1, 32))
    amax = np.abs(blocks).max(-1, keepdims=True)
    byte = np.maximum(np.where(amax > 0, np.frexp(amax)[1] - 1 + 127, 0) - down, 1)
    scale = np.exp2(byte - 127.0)
    codes = (blocks / scale).astype(np.float32).astype(dtype).astype(np.float64)
    return np.moveaxis((codes * scale).reshape(v.shape), -1, axis)


WIDE = False


def mx_kscale(k):
    if not WIDE:
        return np.ones(k)
    levels = np.array([10, -10, 5, -5, 0])
    if k % 512:
        return np.exp2(np.random.permutation(np.resize(levels, k // 32))).repeat(32)
    a = np.empty((k // 512, 16))
    for p in range(k // 512):
        a[p, :8] = np.random.permutation(np.resize(levels, 8))
        for g in range(8):
            far = levels[np.abs(levels - a[p, g]) >= 10]
            a[p, g + 8] = far[np.random.randint(len(far))]
    return np.exp2(a.ravel()).repeat(32)


BF16 = ml_dtypes.bfloat16


def bf(x):
    return np.asarray(x, np.float32).astype(BF16)


def f64(x):
    return np.asarray(x).astype(np.float64)


B, S, M, D, H = 8, 128, 16, 256, 1024


def setup_inputs():
    s = mx_kscale(2 * D)
    lens = np.random.randint(0, M + 1, (B, S))
    valid = (np.arange(M)[None, None, :] < lens[:, :, None]).astype(np.float64)
    src = np.random.standard_normal((B, S, M, D)) / np.sqrt(M) * s[:D]
    neigh = np.random.standard_normal((B, S, M, D)) * 2.0 * valid[..., None] * s[D:]
    return {"src_node_features": bf(src), "neigh_node_features": bf(neigh),
            "W_map": bf(np.random.standard_normal((2 * D, H)) / np.sqrt(2 * D) / s[:, None]),
            "b_map": bf(-0.5 + 0.3 * np.random.standard_normal(H))}


def reference(src_node_features, neigh_node_features, W_map, b_map):
    src, neigh = f64(src_node_features), f64(neigh_node_features)
    valid = np.any(neigh != 0, axis=-1)
    num = np.sum(valid, axis=-1).astype(np.float64)
    neigh_mean = neigh.sum(axis=2) / np.maximum(num, 1.0)[..., None]
    hidden = np.concatenate([src.sum(axis=2), neigh_mean], axis=-1)
    hidden = hidden.reshape(-1, hidden.shape[-1])
    v = (mxq(hidden, 1, "e4m3") @ mxq(f64(W_map), 0, "e4m3")) + f64(b_map)
    return np.where(v >= 0, v, 0.01 * v)

@@ -1,0 +1,372 @@
+from contextlib import ExitStack
+
+import concourse.mybir as mybir
+from concourse.masks import make_identity
+
+F32 = mybir.dt.float32
+BF16 = mybir.dt.bfloat16
+U32 = mybir.dt.uint32
+U8 = mybir.dt.uint8
+I32 = mybir.dt.int32
+FP8X4 = mybir.dt.float8_e4m3fn_x4
+ALU = mybir.AluOpType
+ACT = mybir.ActivationFunctionType
+AXIS = mybir.AxisListType
+
+P = 128
+PACK = 4
+BATCH, NODES, SLOTS, FEAT, HID = 8, 128, 16, 256, 1024
+K = 2 * FEAT
+GROUP_NODES = P // SLOTS
+GROUPS = NODES // GROUP_NODES
+HALF = SLOTS // 2
+N_TILE = 512
+SLOPE = 0.01
+BITS = 0x7FFF7FFF
+VECTOR_ROWS = 4
+SCALAR_ROWS = SLOTS - VECTOR_ROWS
+FOLDED = (0, 1)
+
+FLOPS = 2 * BATCH * NODES * K * HID
+
+
+def tile_syntacticgcn_kernel(tc, src, neigh, w_map, b_map, out):
+    nc = tc.nc
+    with ExitStack() as ctx:
+        const = ctx.enter_context(tc.tile_pool(name="const", bufs=1))
+        loads = ctx.enter_context(tc.tile_pool(name="loads", bufs=1))
+        results = ctx.enter_context(tc.tile_pool(name="results", bufs=BATCH))
+        scratch = ctx.enter_context(tc.tile_pool(name="scratch", bufs=1))
+        work = ctx.enter_context(tc.tile_pool(name="work", bufs=2))
+        psum_hidden = ctx.enter_context(tc.psum_pool(name="psum_hidden", bufs=2))
+        psum_prep = ctx.enter_context(tc.psum_pool(name="psum_prep", bufs=2))
+        psum_out = ctx.enter_context(tc.psum_pool(name="psum_out", bufs=4))
+        ctx.enter_context(tc.manual_schedule())
+
+        raw = {}
+        folded = {}
+        valids = {}
+        counts = {}
+        merged = {}
+        inverses = {}
+        spreads = {}
+        hidden_banks = {}
+        prep_banks = {}
+        grouped_tiles = {}
+        acc_banks = {}
+        result_tiles = {}
+
+        def load(b, which):
+            x = (src, neigh)[which]
+            if b in FOLDED:
+                t = loads.tile([P, SLOTS, FEAT], BF16, name="raw%d_%d" % (b, which))
+                raw[(b, which)] = t
+                for first in range(0, SLOTS, HALF):
+                    slots = slice(first, first + HALF)
+                    nc.sync.dma_start(out=t[:, slots, :], in_=x[b][:, slots, :])
+            else:
+                if b not in raw:
+                    t = loads.tile([P, GROUPS, K], BF16, name="cat%d" % b)
+                    raw[b] = t
+                by_group = x[b].rearrange("(g j) s f -> (j s) g f", j=GROUP_NODES)
+                for first in range(0, GROUPS, GROUPS // 2):
+                    groups = slice(first, first + GROUPS // 2)
+                    nc.sync.dma_start(
+                        out=raw[b][:, groups, which * FEAT : (which + 1) * FEAT],
+                        in_=by_group[:, groups, :],
+                    )
+
+        def count_rows(b, first, last):
+            if first == 0:
+                abs_sum = work.tile([P, SLOTS], F32)
+                counts[b] = abs_sum
+            for r in range(first, last):
+                row = raw[(b, 1)][:, r, :] if b in FOLDED else raw[b][:, r, FEAT:K]
+                abs_values = scratch.tile([P, FEAT], BF16)
+                nc.scalar.activation(
+                    out=abs_values[:], in_=row, func=ACT.Abs, accum_out=counts[b][:, r : r + 1]
+                )
+
+        def merge_rows(b):
+            if b in FOLDED:
+                words = raw[(b, 1)][:].bitcast(I32)[:, SCALAR_ROWS:SLOTS, :]
+            else:
+                words = raw[b][:].bitcast(I32)[:, SCALAR_ROWS:SLOTS, FEAT // 2 : K // 2]
+            width = FEAT // 4
+            half = scratch.tile([P, VECTOR_ROWS, width], I32)
+            quarter = work.tile([P, VECTOR_ROWS, width // 2], I32)
+            nc.vector.tensor_tensor(
+                out=half[:], in0=words[:, :, 0:width], in1=words[:, :, width : 2 * width], op=ALU.bitwise_or
+            )
+            nc.vector.tensor_tensor(
+                out=quarter[:],
+                in0=half[:, :, 0 : width // 2],
+                in1=half[:, :, width // 2 : width],
+                op=ALU.bitwise_or,
+            )
+            merged[b] = quarter
+
+        def reduce_rows(b):
+            quarter = merged[b]
+            unsigned = work.tile([P, VECTOR_ROWS, FEAT // 8], I32)
+            nc.vector.tensor_scalar(
+                out=unsigned[:], in0=quarter[:], scalar1=BITS, scalar2=None, op0=ALU.bitwise_and
+            )
+            nc.vector.tensor_reduce(
+                out=counts[b][:, SCALAR_ROWS:SLOTS], in_=unsigned[:], axis=AXIS.X, op=ALU.max
+            )
+
+        def sign_rows(b):
+            if b in FOLDED:
+                valid = work.tile([P, SLOTS], F32)
+                num = work.tile([P, 1], F32)
+                nc.scalar.activation(out=valid[:], in_=counts[b][:], func=ACT.Sign, accum_out=num[:])
+                counts[b] = num
+            else:
+                valid_bf = work.tile([P, SLOTS], BF16)
+                nc.scalar.activation(out=valid_bf[:], in_=counts[b][:], func=ACT.Sign)
+                valids[b] = valid_bf
+
+        def count_matmul(b):
+            prep = psum_prep.tile([P, 2, P], F32)
+            prep_banks[b] = prep
+            if b not in FOLDED:
+                nc.tensor.matmul(
+                    out=prep[:, 0, 0:GROUPS], lhsT=same_node[:], rhs=valids[b][:], start=True, stop=True
+                )
+
+        def pick_count(b):
+            if b not in FOLDED:
+                picked = work.tile([P, GROUPS], F32)
+                num_node = work.tile([P, 1], F32)
+                nc.vector.scalar_tensor_tensor(
+                    out=picked[:],
+                    in0=prep_banks[b][:, 0, 0:GROUPS],
+                    scalar=1.0,
+                    in1=own_group[:],
+                    op0=ALU.mult,
+                    op1=ALU.mult,
+                    accum_out=num_node[:],
+                )
+                counts[b] = num_node
+            num_floor = work.tile([P, 1], F32)
+            nc.gpsimd.tensor_scalar_max(out=num_floor[:], in0=counts[b][:], scalar1=1.0)
+            counts[b] = num_floor
+
+        def invert_count(b):
+            inv_num = work.tile([P, 1], F32)
+            nc.vector.reciprocal(out=inv_num[:], in_=counts[b][:])
+            spread = spread_tiles[b % 2]
+            nc.gpsimd.tensor_scalar(
+                out=spread[:, P // 2 : P],
+                in0=spread[:, 0 : P // 2],
+                scalar1=inv_num[:, 0:1],
+                scalar2=0.0,
+                op0=ALU.mult,
+                op1=ALU.add,
+            )
+            nc.tensor.transpose(prep_banks[b][:, 1, :], spread[:], identity[:])
+
+        def copy_inverse(b):
+            inverse = work.tile([P, NODES], F32)
+            t = prep_banks[b][:, 1, :]
+            if b in FOLDED:
+                nc.scalar.copy(out=inverse[:], in_=t)
+            else:
+                nc.scalar.copy(
+                    out=inverse[:].rearrange("p (g j) -> p g j", j=GROUP_NODES),
+                    in_=t.rearrange("p (j g) -> p g j", g=GROUPS),
+                )
+            inverses[b] = inverse
+
+        def fold(b, which, first):
+            if b not in folded:
+                half = work.tile([P, HALF, K], F32)
+                folded[b] = half
+            t = raw[(b, which)]
+            quarter = HALF // 2
+            nc.vector.tensor_tensor(
+                out=folded[b][:, first : first + quarter, which * FEAT : (which + 1) * FEAT],
+                in0=t[:, 2 * first : 2 * first + quarter, :],
+                in1=t[:, 2 * first + quarter : 2 * first + 2 * quarter, :],
+                op=ALU.add,
+            )
+
+        def sum_slots(b):
+            hidden_t = psum_hidden.tile([P, PACK, NODES], F32)
+            hidden_banks[b] = hidden_t
+            if b in FOLDED:
+                for t in range(PACK):
+                    for s in range(HALF):
+                        nc.tensor.matmul(
+                            out=hidden_t[:, t, :],
+                            lhsT=folded[b][:, s, t:K:PACK],
+                            rhs=identity[:],
+                            is_transpose=True,
+                            start=(s == 0),
+                            stop=(s == HALF - 1),
+                        )
+            else:
+                for g in range(GROUPS):
+                    for t in range(PACK):
+                        nc.tensor.matmul(
+                            out=hidden_t[:, t, g * GROUP_NODES : (g + 1) * GROUP_NODES],
+                            lhsT=raw[b][:, g, t:K:PACK],
+                            rhs=select[:],
+                            start=True,
+                            stop=True,
+                        )
+
+        def group_hidden(b):
+            grouped = work.tile([P, NODES, PACK], BF16, align_bytes=64)
+            nc.vector.tensor_tensor(
+                out=grouped[:],
+                in0=hidden_banks[b][:].rearrange("p t n -> p n t"),
+                in1=inverses[b][:].unsqueeze(2).to_broadcast([P, NODES, PACK]),
+                op=ALU.mult,
+            )
+            grouped_tiles[b] = grouped
+
+        def quantise_and_multiply(b):
+            h_codes = work.tile([P, NODES], U32, align_bytes=64)
+            h_scales = work.tile([P, NODES], U8, align_bytes=64)
+            nc.vector.quantize_mx(
+                out=h_codes[:].bitcast(FP8X4),
+                scales=h_scales[:],
+                in_=grouped_tiles[b][:].rearrange("p n t -> p (n t)"),
+            )
+            for c in range(HID // N_TILE):
+                cols = slice(c * N_TILE, (c + 1) * N_TILE)
+                acc = psum_out.tile([P, N_TILE], F32)
+                nc.tensor.matmul_mx(
+                    out=acc[:],
+                    lhsT=h_codes[:].bitcast(FP8X4),
+                    lhsT_scale=h_scales[:],
+                    rhs=w_codes[:, cols].bitcast(FP8X4),
+                    rhs_scale=w_scales[:, cols],
+                    start=True,
+                    stop=True,
+                )
+                acc_banks[(b, c)] = acc
+
+        def add_bias(b, c):
+            if c == 0:
+                result = results.tile([P, HID], F32)
+                result_tiles[b] = result
+            cols = slice(c * N_TILE, (c + 1) * N_TILE)
+            nc.vector.tensor_tensor(
+                out=result_tiles[b][:, cols], in0=acc_banks[(b, c)][:], in1=bias[:, cols], op=ALU.add
+            )
+
+        def leaky_and_store(b, c):
+            cols = slice(c * N_TILE, (c + 1) * N_TILE)
+            v = result_tiles[b][:, cols]
+            nc.vector.scalar_tensor_tensor(
+                out=v, in0=v, scalar=SLOPE, in1=v, op0=ALU.mult, op1=ALU.max
+            )
+            nc.sync.dma_start(out=out[b * NODES : (b + 1) * NODES, cols], in_=v)
+
+        w_raw = const.tile([P, PACK, HID], BF16)
+        bias = const.tile([P, HID], BF16)
+        load(0, 1)
+        load(0, 0)
+        nc.sync.dma_start(out=w_raw[:], in_=w_map.rearrange("(p t) n -> p t n", t=PACK))
+        load(1, 1)
+        load(1, 0)
+        nc.sync.dma_start(out=bias[:], in_=b_map.partition_broadcast(P))
+        load(2, 1)
+        for b in range(2, BATCH):
+            if b + 1 < BATCH:
+                load(b + 1, 1)
+            load(b, 0)
+
+        identity = const.tile([P, P], F32)
+        make_identity(nc, identity[:])
+        spread_tiles = []
+        for i in range(2):
+            spread_tile = const.tile([P, P], F32, name="spread%d" % i)
+            nc.gpsimd.memset(spread_tile[:], 1.0)
+            spread_tiles.append(spread_tile)
+        select_f32 = const.tile([P, GROUP_NODES], F32)
+        nc.vector.tensor_reduce(
+            out=select_f32[:],
+            in_=identity[:].rearrange("p (j s) -> p j s", s=SLOTS),
+            axis=AXIS.X,
+            op=ALU.add,
+        )
+        own_group = const.tile([P, GROUPS], F32)
+        nc.vector.tensor_reduce(
+            out=own_group[:],
+            in_=identity[:].rearrange("p (j s) -> p s j", s=GROUPS),
+            axis=AXIS.X,
+            op=ALU.add,
+        )
+        select = const.tile([P, GROUP_NODES], BF16)
+        nc.vector.tensor_copy(out=select[:], in_=select_f32[:])
+        same_node = const.tile([P, P], BF16)
+        nc.vector.tensor_copy(
+            out=same_node[:].rearrange("p (j s) -> p j s", s=SLOTS),
+            in_=select_f32[:].unsqueeze(2).to_broadcast([P, GROUP_NODES, SLOTS]),
+        )
+        w_grouped = const.tile([P, HID, PACK], BF16, align_bytes=64)
+        w_codes = const.tile([P, HID], U32, align_bytes=64)
+        w_scales = const.tile([P, HID], U8, align_bytes=64)
+
+        def prepare_weights(c):
+            cols = slice(c * N_TILE, (c + 1) * N_TILE)
+            nc.vector.tensor_copy(
+                out=w_grouped[:, cols, :], in_=w_raw[:, :, cols].rearrange("p t n -> p n t")
+            )
+
+        def quantise_weights():
+            nc.vector.quantize_mx(
+                out=w_codes[:].bitcast(FP8X4),
+                scales=w_scales[:],
+                in_=w_grouped[:].rearrange("p n t -> p (n t)"),
+            )
+
+        def folds(b, which, first):
+            if b in FOLDED:
+                fold(b, which, first)
+
+        for m in range(BATCH + 2):
+            counting = m < BATCH
+            dividing = 1 <= m <= BATCH
+            finishing = m >= 2
+            if counting:
+                count_rows(m, 0, HALF)
+            if dividing:
+                count_matmul(m - 1)
+                pick_count(m - 1)
+            if finishing:
+                quantise_and_multiply(m - 2)
+            if counting:
+                folds(m, 1, 0)
+                merge_rows(m)
+            if dividing:
+                invert_count(m - 1)
+                copy_inverse(m - 1)
+            if counting:
+                reduce_rows(m)
+                count_rows(m, HALF, SCALAR_ROWS)
+                sign_rows(m)
+            if finishing:
+                add_bias(m - 2, 0)
+                add_bias(m - 2, 1)
+            if counting:
+                folds(m, 1, HALF // 2)
+            if finishing:
+                leaky_and_store(m - 2, 0)
+            if m == 1:
+                prepare_weights(0)
+                prepare_weights(1)
+            if dividing:
+                group_hidden(m - 1)
+            if finishing:
+                leaky_and_store(m - 2, 1)
+            if m == 1:
+                quantise_weights()
+            if counting:
+                folds(m, 0, 0)
+                folds(m, 0, HALF // 2)
+                sum_slots(m)

@@ -17,6 +17,7 @@ P = 128
 PACK = 4
 BATCH, NODES, SLOTS, FEAT, HID = 8, 128, 16, 256, 1024
 K = 2 * FEAT
+CHUNKS = K // P
 GROUP_NODES = P // SLOTS
 GROUPS = NODES // GROUP_NODES
 HALF = SLOTS // 2
@@ -38,9 +39,11 @@ def tile_syntacticgcn_kernel(tc, src, neigh, w_map, b_map, out):
         results = ctx.enter_context(tc.tile_pool(name="results", bufs=BATCH))
         scratch = ctx.enter_context(tc.tile_pool(name="scratch", bufs=1))
         work = ctx.enter_context(tc.tile_pool(name="work", bufs=2))
+        psum_sums = ctx.enter_context(tc.psum_pool(name="psum_sums", bufs=1))
+        psum_turned = ctx.enter_context(tc.psum_pool(name="psum_turned", bufs=1))
         psum_hidden = ctx.enter_context(tc.psum_pool(name="psum_hidden", bufs=2))
-        psum_prep = ctx.enter_context(tc.psum_pool(name="psum_prep", bufs=2))
-        psum_out = ctx.enter_context(tc.psum_pool(name="psum_out", bufs=4))
+        psum_prep = ctx.enter_context(tc.psum_pool(name="psum_prep", bufs=1))
+        psum_out = ctx.enter_context(tc.psum_pool(name="psum_out", bufs=3))
         ctx.enter_context(tc.manual_schedule())
 
         raw = {}
@@ -49,7 +52,8 @@ def tile_syntacticgcn_kernel(tc, src, neigh, w_map, b_map, out):
         counts = {}
         merged = {}
         inverses = {}
-        spreads = {}
+        sum_banks = {}
+        turned_banks = {}
         hidden_banks = {}
         prep_banks = {}
         grouped_tiles = {}
@@ -125,107 +129,137 @@ def tile_syntacticgcn_kernel(tc, src, neigh, w_map, b_map, out):
             else:
                 valid_bf = work.tile([P, SLOTS], BF16)
                 nc.scalar.activation(out=valid_bf[:], in_=counts[b][:], func=ACT.Sign)
-                valids[b] = valid_bf
+                own_valid = work.tile([P, GROUPS, GROUP_NODES], BF16)
+                nc.gpsimd.tensor_tensor(
+                    out=own_valid[:],
+                    in0=valid_bf[:].unsqueeze(2).to_broadcast([P, GROUPS, GROUP_NODES]),
+                    in1=select[:].unsqueeze(1).to_broadcast([P, GROUPS, GROUP_NODES]),
+                    op=ALU.mult,
+                )
+                valids[b] = own_valid
 
         def count_matmul(b):
-            prep = psum_prep.tile([P, 2, P], F32)
+            prep = psum_prep.tile([P, P], F32)
             prep_banks[b] = prep
             if b not in FOLDED:
                 nc.tensor.matmul(
-                    out=prep[:, 0, 0:GROUPS], lhsT=same_node[:], rhs=valids[b][:], start=True, stop=True
+                    out=prep[:, 0:1],
+                    lhsT=valids[b][:].rearrange("p g j -> p (g j)"),
+                    rhs=ones[:],
+                    start=True,
+                    stop=True,
                 )
 
-        def pick_count(b):
-            if b not in FOLDED:
-                picked = work.tile([P, GROUPS], F32)
-                num_node = work.tile([P, 1], F32)
-                nc.vector.scalar_tensor_tensor(
-                    out=picked[:],
-                    in0=prep_banks[b][:, 0, 0:GROUPS],
-                    scalar=1.0,
-                    in1=own_group[:],
-                    op0=ALU.mult,
-                    op1=ALU.mult,
-                    accum_out=num_node[:],
-                )
-                counts[b] = num_node
+        def clamp_count(b):
             num_floor = work.tile([P, 1], F32)
-            nc.gpsimd.tensor_scalar_max(out=num_floor[:], in0=counts[b][:], scalar1=1.0)
+            num = counts[b][:] if b in FOLDED else prep_banks[b][:, 0:1]
+            nc.vector.tensor_scalar_max(out=num_floor[:], in0=num, scalar1=1.0)
             counts[b] = num_floor
 
         def invert_count(b):
-            inv_num = work.tile([P, 1], F32)
-            nc.vector.reciprocal(out=inv_num[:], in_=counts[b][:])
-            spread = spread_tiles[b % 2]
-            nc.gpsimd.tensor_scalar(
-                out=spread[:, P // 2 : P],
-                in0=spread[:, 0 : P // 2],
-                scalar1=inv_num[:, 0:1],
-                scalar2=0.0,
-                op0=ALU.mult,
-                op1=ALU.add,
-            )
-            nc.tensor.transpose(prep_banks[b][:, 1, :], spread[:], identity[:])
+            if b in FOLDED:
+                inv_num = work.tile([P, 1], F32)
+                nc.vector.reciprocal(out=inv_num[:], in_=counts[b][:])
+                spread = spread_tiles[b % 2]
+                nc.gpsimd.tensor_scalar(
+                    out=spread[:, P // 2 : P],
+                    in0=spread[:, 0 : P // 2],
+                    scalar1=inv_num[:, 0:1],
+                    scalar2=0.0,
+                    op0=ALU.mult,
+                    op1=ALU.add,
+                )
+                nc.tensor.transpose(prep_banks[b][:], spread[:], identity[:])
+            else:
+                nc.vector.reciprocal(out=factor_tiles[b % 2][:, 1:2], in_=counts[b][:])
 
         def copy_inverse(b):
-            inverse = work.tile([P, NODES], F32)
-            t = prep_banks[b][:, 1, :]
             if b in FOLDED:
-                nc.scalar.copy(out=inverse[:], in_=t)
-            else:
-                nc.scalar.copy(
-                    out=inverse[:].rearrange("p (g j) -> p g j", j=GROUP_NODES),
-                    in_=t.rearrange("p (j g) -> p g j", g=GROUPS),
-                )
-            inverses[b] = inverse
+                inverse = work.tile([P, NODES], F32)
+                nc.scalar.copy(out=inverse[:], in_=prep_banks[b][:])
+                inverses[b] = inverse
 
         def fold(b, which, first):
             if b not in folded:
-                half = work.tile([P, HALF, K], F32)
-                folded[b] = half
+                half_sums = work.tile([P, HALF, PACK, P], F32)
+                folded[b] = half_sums
             t = raw[(b, which)]
             quarter = HALF // 2
-            nc.vector.tensor_tensor(
-                out=folded[b][:, first : first + quarter, which * FEAT : (which + 1) * FEAT],
-                in0=t[:, 2 * first : 2 * first + quarter, :],
-                in1=t[:, 2 * first + quarter : 2 * first + 2 * quarter, :],
-                op=ALU.add,
-            )
+            rows = slice(which * P // 2, (which + 1) * P // 2)
+            for s in range(quarter):
+                nc.vector.tensor_tensor(
+                    out=folded[b][:, first + s, :, rows],
+                    in0=t[:, 2 * first + s, :].rearrange("p (m t) -> p t m", t=PACK),
+                    in1=t[:, 2 * first + quarter + s, :].rearrange("p (m t) -> p t m", t=PACK),
+                    op=ALU.add,
+                )
 
         def sum_slots(b):
-            hidden_t = psum_hidden.tile([P, PACK, NODES], F32)
-            hidden_banks[b] = hidden_t
             if b in FOLDED:
+                hidden_t = psum_hidden.tile([P, PACK, NODES], F32)
+                hidden_banks[b] = hidden_t
                 for t in range(PACK):
                     for s in range(HALF):
                         nc.tensor.matmul(
                             out=hidden_t[:, t, :],
-                            lhsT=folded[b][:, s, t:K:PACK],
+                            lhsT=folded[b][:, s, t, :],
                             rhs=identity[:],
                             is_transpose=True,
                             start=(s == 0),
                             stop=(s == HALF - 1),
                         )
             else:
+                sums_t = psum_sums.tile([P, CHUNKS, NODES], F32)
+                sum_banks[b] = sums_t
                 for g in range(GROUPS):
-                    for t in range(PACK):
+                    for c in range(CHUNKS):
                         nc.tensor.matmul(
-                            out=hidden_t[:, t, g * GROUP_NODES : (g + 1) * GROUP_NODES],
-                            lhsT=raw[b][:, g, t:K:PACK],
+                            out=sums_t[:, c, g * GROUP_NODES : (g + 1) * GROUP_NODES],
+                            lhsT=raw[b][:, g, c * P : (c + 1) * P],
                             rhs=select[:],
                             start=True,
                             stop=True,
                         )
 
+        def turn_sums(b):
+            if b in FOLDED:
+                return
+            sums = work.tile([P, CHUNKS, NODES], F32)
+            nc.scalar.copy(out=sums[:], in_=sum_banks[b][:])
+            turned = psum_turned.tile([P, K], F32)
+            for c in range(CHUNKS):
+                nc.tensor.transpose(turned[:, c * P : (c + 1) * P], sums[:, c, :], identity[:])
+            turned_banks[b] = turned
+
+        def divide(b):
+            if b in FOLDED:
+                grouped = work.tile([P, NODES, PACK], BF16, align_bytes=64)
+                nc.vector.tensor_tensor(
+                    out=grouped[:],
+                    in0=hidden_banks[b][:].rearrange("p t n -> p n t"),
+                    in1=inverses[b][:].unsqueeze(2).to_broadcast([P, NODES, PACK]),
+                    op=ALU.mult,
+                )
+                grouped_tiles[b] = grouped
+            else:
+                hidden = work.tile([P, 2, FEAT], F32)
+                nc.vector.tensor_tensor(
+                    out=hidden[:],
+                    in0=turned_banks[b][:].rearrange("p (w f) -> p w f", w=2),
+                    in1=factor_tiles[b % 2][:].unsqueeze(2).to_broadcast([P, 2, FEAT]),
+                    op=ALU.mult,
+                )
+                hidden_t = psum_hidden.tile([P, PACK, NODES], F32)
+                flat = hidden[:].rearrange("p w f -> p (w f)")
+                for t in range(PACK):
+                    nc.tensor.transpose(hidden_t[:, t, :], flat[:, t:K:PACK], identity[:])
+                hidden_banks[b] = hidden_t
+
         def group_hidden(b):
-            grouped = work.tile([P, NODES, PACK], BF16, align_bytes=64)
-            nc.vector.tensor_tensor(
-                out=grouped[:],
-                in0=hidden_banks[b][:].rearrange("p t n -> p n t"),
-                in1=inverses[b][:].unsqueeze(2).to_broadcast([P, NODES, PACK]),
-                op=ALU.mult,
-            )
-            grouped_tiles[b] = grouped
+            if b not in FOLDED:
+                grouped = work.tile([P, NODES, PACK], BF16, align_bytes=64)
+                nc.scalar.copy(out=grouped[:], in_=hidden_banks[b][:].rearrange("p t n -> p n t"))
+                grouped_tiles[b] = grouped
 
         def quantise_and_multiply(b):
             h_codes = work.tile([P, NODES], U32, align_bytes=64)
@@ -270,11 +304,11 @@ def tile_syntacticgcn_kernel(tc, src, neigh, w_map, b_map, out):
         bias = const.tile([P, HID], BF16)
         load(0, 1)
         load(0, 0)
-        nc.sync.dma_start(out=w_raw[:], in_=w_map.rearrange("(p t) n -> p t n", t=PACK))
         load(1, 1)
+        load(2, 1)
+        nc.sync.dma_start(out=w_raw[:], in_=w_map.rearrange("(p t) n -> p t n", t=PACK))
         load(1, 0)
         nc.sync.dma_start(out=bias[:], in_=b_map.partition_broadcast(P))
-        load(2, 1)
         for b in range(2, BATCH):
             if b + 1 < BATCH:
                 load(b + 1, 1)
@@ -283,10 +317,16 @@ def tile_syntacticgcn_kernel(tc, src, neigh, w_map, b_map, out):
         identity = const.tile([P, P], F32)
         make_identity(nc, identity[:])
         spread_tiles = []
+        factor_tiles = []
         for i in range(2):
             spread_tile = const.tile([P, P], F32, name="spread%d" % i)
+            factor_tile = const.tile([P, 2], F32, name="factor%d" % i)
             nc.gpsimd.memset(spread_tile[:], 1.0)
+            nc.gpsimd.memset(factor_tile[:], 1.0)
             spread_tiles.append(spread_tile)
+            factor_tiles.append(factor_tile)
+        ones = const.tile([P, 1], BF16)
+        nc.gpsimd.memset(ones[:], 1.0)
         select_f32 = const.tile([P, GROUP_NODES], F32)
         nc.vector.tensor_reduce(
             out=select_f32[:],
@@ -294,20 +334,8 @@ def tile_syntacticgcn_kernel(tc, src, neigh, w_map, b_map, out):
             axis=AXIS.X,
             op=ALU.add,
         )
-        own_group = const.tile([P, GROUPS], F32)
-        nc.vector.tensor_reduce(
-            out=own_group[:],
-            in_=identity[:].rearrange("p (j s) -> p s j", s=GROUPS),
-            axis=AXIS.X,
-            op=ALU.add,
-        )
         select = const.tile([P, GROUP_NODES], BF16)
         nc.vector.tensor_copy(out=select[:], in_=select_f32[:])
-        same_node = const.tile([P, P], BF16)
-        nc.vector.tensor_copy(
-            out=same_node[:].rearrange("p (j s) -> p j s", s=SLOTS),
-            in_=select_f32[:].unsqueeze(2).to_broadcast([P, GROUP_NODES, SLOTS]),
-        )
         w_grouped = const.tile([P, HID, PACK], BF16, align_bytes=64)
         w_codes = const.tile([P, HID], U32, align_bytes=64)
         w_scales = const.tile([P, HID], U8, align_bytes=64)
@@ -325,48 +353,48 @@ def tile_syntacticgcn_kernel(tc, src, neigh, w_map, b_map, out):
                 in_=w_grouped[:].rearrange("p n t -> p (n t)"),
             )
 
-        def folds(b, which, first):
+        def folds(b, which):
             if b in FOLDED:
-                fold(b, which, first)
+                fold(b, which, 0)
+                fold(b, which, HALF // 2)
 
         for m in range(BATCH + 2):
             counting = m < BATCH
             dividing = 1 <= m <= BATCH
             finishing = m >= 2
-            if counting:
-                count_rows(m, 0, HALF)
-            if dividing:
-                count_matmul(m - 1)
-                pick_count(m - 1)
             if finishing:
                 quantise_and_multiply(m - 2)
+            if dividing:
+                turn_sums(m - 1)
             if counting:
-                folds(m, 1, 0)
+                count_rows(m, 0, SCALAR_ROWS)
                 merge_rows(m)
+                folds(m, 1)
+            if dividing:
+                count_matmul(m - 1)
+            if finishing:
+                add_bias(m - 2, 0)
+            if dividing:
+                clamp_count(m - 1)
+            if finishing:
+                add_bias(m - 2, 1)
             if dividing:
                 invert_count(m - 1)
+            if finishing:
+                leaky_and_store(m - 2, 0)
+            if dividing:
                 copy_inverse(m - 1)
             if counting:
                 reduce_rows(m)
-                count_rows(m, HALF, SCALAR_ROWS)
                 sign_rows(m)
-            if finishing:
-                add_bias(m - 2, 0)
-                add_bias(m - 2, 1)
-            if counting:
-                folds(m, 1, HALF // 2)
-            if finishing:
-                leaky_and_store(m - 2, 0)
+                folds(m, 0)
+                sum_slots(m)
+            if dividing:
+                divide(m - 1)
+                group_hidden(m - 1)
             if m == 1:
                 prepare_weights(0)
                 prepare_weights(1)
-            if dividing:
-                group_hidden(m - 1)
+                quantise_weights()
             if finishing:
                 leaky_and_store(m - 2, 1)
-            if m == 1:
-                quantise_weights()
-            if counting:
-                folds(m, 0, 0)
-                folds(m, 0, HALF // 2)
-                sum_slots(m)

@@ -24,9 +24,8 @@ HALF = SLOTS // 2
 N_TILE = 512
 SLOPE = 0.01
 BITS = 0x7FFF7FFF
-VECTOR_ROWS = 4
-SCALAR_ROWS = SLOTS - VECTOR_ROWS
 FOLDED = (0, 1)
+VECTOR_ROWS = 6
 
 FLOPS = 2 * BATCH * NODES * K * HID
 
@@ -35,70 +34,72 @@ def tile_syntacticgcn_kernel(tc, src, neigh, w_map, b_map, out):
     nc = tc.nc
     with ExitStack() as ctx:
         const = ctx.enter_context(tc.tile_pool(name="const", bufs=1))
-        loads = ctx.enter_context(tc.tile_pool(name="loads", bufs=1))
+        loads = ctx.enter_context(tc.tile_pool(name="loads", bufs=BATCH))
         results = ctx.enter_context(tc.tile_pool(name="results", bufs=BATCH))
         scratch = ctx.enter_context(tc.tile_pool(name="scratch", bufs=1))
         work = ctx.enter_context(tc.tile_pool(name="work", bufs=2))
-        psum_sums = ctx.enter_context(tc.psum_pool(name="psum_sums", bufs=1))
+        psum_sums = ctx.enter_context(tc.psum_pool(name="psum_sums", bufs=2))
         psum_turned = ctx.enter_context(tc.psum_pool(name="psum_turned", bufs=1))
-        psum_hidden = ctx.enter_context(tc.psum_pool(name="psum_hidden", bufs=2))
-        psum_prep = ctx.enter_context(tc.psum_pool(name="psum_prep", bufs=1))
+        psum_hidden = ctx.enter_context(tc.psum_pool(name="psum_hidden", bufs=1))
+        psum_num = ctx.enter_context(tc.psum_pool(name="psum_num", bufs=1))
         psum_out = ctx.enter_context(tc.psum_pool(name="psum_out", bufs=3))
         ctx.enter_context(tc.manual_schedule())
 
         raw = {}
         folded = {}
+        abs_sums = {}
+        abs_values = {}
+        merged = {}
         valids = {}
         counts = {}
-        merged = {}
         inverses = {}
         sum_banks = {}
+        sums_tiles = {}
         turned_banks = {}
+        hidden_tiles = {}
         hidden_banks = {}
-        prep_banks = {}
         grouped_tiles = {}
+        code_tiles = {}
         acc_banks = {}
         result_tiles = {}
 
         def load(b, which):
             x = (src, neigh)[which]
+            t = loads.tile([P, SLOTS, FEAT], BF16, name="raw%d" % which)
+            raw[(b, which)] = t
             if b in FOLDED:
-                t = loads.tile([P, SLOTS, FEAT], BF16, name="raw%d_%d" % (b, which))
-                raw[(b, which)] = t
-                for first in range(0, SLOTS, HALF):
-                    slots = slice(first, first + HALF)
-                    nc.sync.dma_start(out=t[:, slots, :], in_=x[b][:, slots, :])
+                rows = x[b]
             else:
-                if b not in raw:
-                    t = loads.tile([P, GROUPS, K], BF16, name="cat%d" % b)
-                    raw[b] = t
-                by_group = x[b].rearrange("(g j) s f -> (j s) g f", j=GROUP_NODES)
-                for first in range(0, GROUPS, GROUPS // 2):
-                    groups = slice(first, first + GROUPS // 2)
-                    nc.sync.dma_start(
-                        out=raw[b][:, groups, which * FEAT : (which + 1) * FEAT],
-                        in_=by_group[:, groups, :],
-                    )
+                rows = x[b].rearrange("(g j) s f -> (j s) g f", j=GROUP_NODES)
+            for first in range(0, SLOTS, HALF):
+                half = slice(first, first + HALF)
+                nc.sync.dma_start(out=t[:, half, :], in_=rows[:, half, :])
+
+        def vector_rows(b):
+            return 0 if b in FOLDED else VECTOR_ROWS
 
         def count_rows(b, first, last):
             if first == 0:
                 abs_sum = work.tile([P, SLOTS], F32)
-                counts[b] = abs_sum
-            for r in range(first, last):
-                row = raw[(b, 1)][:, r, :] if b in FOLDED else raw[b][:, r, FEAT:K]
-                abs_values = scratch.tile([P, FEAT], BF16)
+                abs_sums[b] = abs_sum
+                abs_tile = scratch.tile([P, SLOTS, FEAT], BF16)
+                abs_values[b] = abs_tile
+            for r in range(first, min(last, SLOTS - vector_rows(b))):
                 nc.scalar.activation(
-                    out=abs_values[:], in_=row, func=ACT.Abs, accum_out=counts[b][:, r : r + 1]
+                    out=abs_values[b][:, r, :],
+                    in_=raw[(b, 1)][:, r, :],
+                    func=ACT.Abs,
+                    accum_out=abs_sums[b][:, r : r + 1],
                 )
 
         def merge_rows(b):
-            if b in FOLDED:
-                words = raw[(b, 1)][:].bitcast(I32)[:, SCALAR_ROWS:SLOTS, :]
-            else:
-                words = raw[b][:].bitcast(I32)[:, SCALAR_ROWS:SLOTS, FEAT // 2 : K // 2]
+            rows = vector_rows(b)
+            if rows == 0:
+                return
+            words = raw[(b, 1)][:].bitcast(I32)[:, SLOTS - rows : SLOTS, :]
             width = FEAT // 4
-            half = scratch.tile([P, VECTOR_ROWS, width], I32)
-            quarter = work.tile([P, VECTOR_ROWS, width // 2], I32)
+            half = scratch.tile([P, rows, width], I32)
+            quarter = work.tile([P, rows, width // 2], I32)
             nc.vector.tensor_tensor(
                 out=half[:], in0=words[:, :, 0:width], in1=words[:, :, width : 2 * width], op=ALU.bitwise_or
             )
@@ -111,24 +112,26 @@ def tile_syntacticgcn_kernel(tc, src, neigh, w_map, b_map, out):
             merged[b] = quarter
 
         def reduce_rows(b):
-            quarter = merged[b]
-            unsigned = work.tile([P, VECTOR_ROWS, FEAT // 8], I32)
+            rows = vector_rows(b)
+            if rows == 0:
+                return
+            unsigned = work.tile([P, rows, FEAT // 8], I32)
             nc.vector.tensor_scalar(
-                out=unsigned[:], in0=quarter[:], scalar1=BITS, scalar2=None, op0=ALU.bitwise_and
+                out=unsigned[:], in0=merged[b][:], scalar1=BITS, scalar2=None, op0=ALU.bitwise_and
             )
             nc.vector.tensor_reduce(
-                out=counts[b][:, SCALAR_ROWS:SLOTS], in_=unsigned[:], axis=AXIS.X, op=ALU.max
+                out=abs_sums[b][:, SLOTS - rows : SLOTS], in_=unsigned[:], axis=AXIS.X, op=ALU.max
             )
 
         def sign_rows(b):
             if b in FOLDED:
                 valid = work.tile([P, SLOTS], F32)
                 num = work.tile([P, 1], F32)
-                nc.scalar.activation(out=valid[:], in_=counts[b][:], func=ACT.Sign, accum_out=num[:])
+                nc.scalar.activation(out=valid[:], in_=abs_sums[b][:], func=ACT.Sign, accum_out=num[:])
                 counts[b] = num
             else:
-                valid_bf = work.tile([P, SLOTS], BF16)
-                nc.scalar.activation(out=valid_bf[:], in_=counts[b][:], func=ACT.Sign)
+                valid_bf = work.tile([P, GROUPS], BF16)
+                nc.scalar.activation(out=valid_bf[:], in_=abs_sums[b][:], func=ACT.Sign)
                 own_valid = work.tile([P, GROUPS, GROUP_NODES], BF16)
                 nc.gpsimd.tensor_tensor(
                     out=own_valid[:],
@@ -139,136 +142,117 @@ def tile_syntacticgcn_kernel(tc, src, neigh, w_map, b_map, out):
                 valids[b] = own_valid
 
         def count_matmul(b):
-            prep = psum_prep.tile([P, P], F32)
-            prep_banks[b] = prep
             if b not in FOLDED:
+                num_t = psum_num.tile([P, 1], F32)
                 nc.tensor.matmul(
-                    out=prep[:, 0:1],
+                    out=num_t[:],
                     lhsT=valids[b][:].rearrange("p g j -> p (g j)"),
                     rhs=ones[:],
                     start=True,
                     stop=True,
                 )
+                counts[b] = num_t
 
         def clamp_count(b):
             num_floor = work.tile([P, 1], F32)
-            num = counts[b][:] if b in FOLDED else prep_banks[b][:, 0:1]
-            nc.vector.tensor_scalar_max(out=num_floor[:], in0=num, scalar1=1.0)
+            nc.vector.tensor_scalar_max(out=num_floor[:], in0=counts[b][:], scalar1=1.0)
             counts[b] = num_floor
 
         def invert_count(b):
-            if b in FOLDED:
-                inv_num = work.tile([P, 1], F32)
-                nc.vector.reciprocal(out=inv_num[:], in_=counts[b][:])
-                spread = spread_tiles[b % 2]
-                nc.gpsimd.tensor_scalar(
-                    out=spread[:, P // 2 : P],
-                    in0=spread[:, 0 : P // 2],
-                    scalar1=inv_num[:, 0:1],
-                    scalar2=0.0,
-                    op0=ALU.mult,
-                    op1=ALU.add,
-                )
-                nc.tensor.transpose(prep_banks[b][:], spread[:], identity[:])
-            else:
-                nc.vector.reciprocal(out=factor_tiles[b % 2][:, 1:2], in_=counts[b][:])
+            inv_num = work.tile([P, 1], F32)
+            nc.vector.reciprocal(out=inv_num[:], in_=counts[b][:])
+            inverses[b] = inv_num
 
-        def copy_inverse(b):
-            if b in FOLDED:
-                inverse = work.tile([P, NODES], F32)
-                nc.scalar.copy(out=inverse[:], in_=prep_banks[b][:])
-                inverses[b] = inverse
-
-        def fold(b, which, first):
-            if b not in folded:
-                half_sums = work.tile([P, HALF, PACK, P], F32)
-                folded[b] = half_sums
-            t = raw[(b, which)]
+        def fold(b, which, part):
+            if b not in FOLDED:
+                return
+            if part == 0:
+                pair_sums = scratch.tile([P, HALF, FEAT], F32, name="pairs%d" % which)
+                folded[(b, which)] = pair_sums
             quarter = HALF // 2
-            rows = slice(which * P // 2, (which + 1) * P // 2)
-            for s in range(quarter):
-                nc.vector.tensor_tensor(
-                    out=folded[b][:, first + s, :, rows],
-                    in0=t[:, 2 * first + s, :].rearrange("p (m t) -> p t m", t=PACK),
-                    in1=t[:, 2 * first + quarter + s, :].rearrange("p (m t) -> p t m", t=PACK),
-                    op=ALU.add,
-                )
+            first = part * HALF
+            nc.vector.tensor_tensor(
+                out=folded[(b, which)][:, part * quarter : (part + 1) * quarter, :],
+                in0=raw[(b, which)][:, first : first + quarter, :],
+                in1=raw[(b, which)][:, first + quarter : first + HALF, :],
+                op=ALU.add,
+            )
 
-        def sum_slots(b):
+        def sum_slots(b, which):
+            if b not in sum_banks:
+                sums_t = psum_sums.tile([P, CHUNKS, NODES], F32)
+                sum_banks[b] = sums_t
+            chunks = range(which * CHUNKS // 2, (which + 1) * CHUNKS // 2)
             if b in FOLDED:
-                hidden_t = psum_hidden.tile([P, PACK, NODES], F32)
-                hidden_banks[b] = hidden_t
-                for t in range(PACK):
+                for c in chunks:
+                    first = c * P - which * FEAT
                     for s in range(HALF):
                         nc.tensor.matmul(
-                            out=hidden_t[:, t, :],
-                            lhsT=folded[b][:, s, t, :],
+                            out=sum_banks[b][:, c, :],
+                            lhsT=folded[(b, which)][:, s, first : first + P],
                             rhs=identity[:],
                             is_transpose=True,
                             start=(s == 0),
                             stop=(s == HALF - 1),
                         )
             else:
-                sums_t = psum_sums.tile([P, CHUNKS, NODES], F32)
-                sum_banks[b] = sums_t
                 for g in range(GROUPS):
-                    for c in range(CHUNKS):
+                    for c in chunks:
                         nc.tensor.matmul(
-                            out=sums_t[:, c, g * GROUP_NODES : (g + 1) * GROUP_NODES],
-                            lhsT=raw[b][:, g, c * P : (c + 1) * P],
+                            out=sum_banks[b][:, c, g * GROUP_NODES : (g + 1) * GROUP_NODES],
+                            lhsT=raw[(b, which)][:, g, c * P - which * FEAT : (c + 1) * P - which * FEAT],
                             rhs=select[:],
                             start=True,
                             stop=True,
                         )
 
-        def turn_sums(b):
-            if b in FOLDED:
-                return
+        def copy_sums(b):
             sums = work.tile([P, CHUNKS, NODES], F32)
             nc.scalar.copy(out=sums[:], in_=sum_banks[b][:])
+            sums_tiles[b] = sums
+
+        def turn_sums(b):
             turned = psum_turned.tile([P, K], F32)
             for c in range(CHUNKS):
-                nc.tensor.transpose(turned[:, c * P : (c + 1) * P], sums[:, c, :], identity[:])
+                nc.tensor.transpose(turned[:, c * P : (c + 1) * P], sums_tiles[b][:, c, :], identity[:])
             turned_banks[b] = turned
 
         def divide(b):
-            if b in FOLDED:
-                grouped = work.tile([P, NODES, PACK], BF16, align_bytes=64)
-                nc.vector.tensor_tensor(
-                    out=grouped[:],
-                    in0=hidden_banks[b][:].rearrange("p t n -> p n t"),
-                    in1=inverses[b][:].unsqueeze(2).to_broadcast([P, NODES, PACK]),
-                    op=ALU.mult,
-                )
-                grouped_tiles[b] = grouped
-            else:
-                hidden = work.tile([P, 2, FEAT], F32)
-                nc.vector.tensor_tensor(
-                    out=hidden[:],
-                    in0=turned_banks[b][:].rearrange("p (w f) -> p w f", w=2),
-                    in1=factor_tiles[b % 2][:].unsqueeze(2).to_broadcast([P, 2, FEAT]),
-                    op=ALU.mult,
-                )
-                hidden_t = psum_hidden.tile([P, PACK, NODES], F32)
-                flat = hidden[:].rearrange("p w f -> p (w f)")
-                for t in range(PACK):
-                    nc.tensor.transpose(hidden_t[:, t, :], flat[:, t:K:PACK], identity[:])
-                hidden_banks[b] = hidden_t
+            hidden = work.tile([P, K], BF16)
+            nc.scalar.copy(out=hidden[:, 0:FEAT], in_=turned_banks[b][:, 0:FEAT])
+            nc.scalar.activation(
+                out=hidden[:, FEAT:K],
+                in_=turned_banks[b][:, FEAT:K],
+                func=ACT.Copy,
+                scale=inverses[b][:, 0:1],
+            )
+            hidden_tiles[b] = hidden
+
+        def turn_hidden(b):
+            hidden_t = psum_hidden.tile([P, PACK // 2, NODES], F32)
+            words = hidden_tiles[b][:].bitcast(F32)
+            for u in range(PACK // 2):
+                nc.tensor.transpose(hidden_t[:, u, :], words[:, u : K // 2 : PACK // 2], identity[:])
+            hidden_banks[b] = hidden_t
 
         def group_hidden(b):
-            if b not in FOLDED:
-                grouped = work.tile([P, NODES, PACK], BF16, align_bytes=64)
-                nc.scalar.copy(out=grouped[:], in_=hidden_banks[b][:].rearrange("p t n -> p n t"))
-                grouped_tiles[b] = grouped
+            grouped = work.tile([P, NODES * PACK], BF16, align_bytes=64)
+            nc.scalar.copy(
+                out=grouped[:].bitcast(F32).rearrange("p (n u) -> p n u", u=PACK // 2),
+                in_=hidden_banks[b][:].rearrange("p u n -> p n u"),
+            )
+            grouped_tiles[b] = grouped
 
-        def quantise_and_multiply(b):
+        def quantise(b):
             h_codes = work.tile([P, NODES], U32, align_bytes=64)
             h_scales = work.tile([P, NODES], U8, align_bytes=64)
             nc.vector.quantize_mx(
-                out=h_codes[:].bitcast(FP8X4),
-                scales=h_scales[:],
-                in_=grouped_tiles[b][:].rearrange("p n t -> p (n t)"),
+                out=h_codes[:].bitcast(FP8X4), scales=h_scales[:], in_=grouped_tiles[b][:]
             )
+            code_tiles[b] = (h_codes, h_scales)
+
+        def multiply(b):
+            h_codes, h_scales = code_tiles[b]
             for c in range(HID // N_TILE):
                 cols = slice(c * N_TILE, (c + 1) * N_TILE)
                 acc = psum_out.tile([P, N_TILE], F32)
@@ -305,26 +289,19 @@ def tile_syntacticgcn_kernel(tc, src, neigh, w_map, b_map, out):
         load(0, 1)
         load(0, 0)
         load(1, 1)
-        load(2, 1)
-        nc.sync.dma_start(out=w_raw[:], in_=w_map.rearrange("(p t) n -> p t n", t=PACK))
         load(1, 0)
+        nc.sync.dma_start(out=w_raw[:], in_=w_map.rearrange("(p t) n -> p t n", t=PACK))
+        load(2, 1)
+        load(3, 1)
+        load(2, 0)
         nc.sync.dma_start(out=bias[:], in_=b_map.partition_broadcast(P))
-        for b in range(2, BATCH):
+        for b in range(3, BATCH):
             if b + 1 < BATCH:
                 load(b + 1, 1)
             load(b, 0)
 
         identity = const.tile([P, P], F32)
         make_identity(nc, identity[:])
-        spread_tiles = []
-        factor_tiles = []
-        for i in range(2):
-            spread_tile = const.tile([P, P], F32, name="spread%d" % i)
-            factor_tile = const.tile([P, 2], F32, name="factor%d" % i)
-            nc.gpsimd.memset(spread_tile[:], 1.0)
-            nc.gpsimd.memset(factor_tile[:], 1.0)
-            spread_tiles.append(spread_tile)
-            factor_tiles.append(factor_tile)
         ones = const.tile([P, 1], BF16)
         nc.gpsimd.memset(ones[:], 1.0)
         select_f32 = const.tile([P, GROUP_NODES], F32)
@@ -340,61 +317,68 @@ def tile_syntacticgcn_kernel(tc, src, neigh, w_map, b_map, out):
         w_codes = const.tile([P, HID], U32, align_bytes=64)
         w_scales = const.tile([P, HID], U8, align_bytes=64)
 
-        def prepare_weights(c):
-            cols = slice(c * N_TILE, (c + 1) * N_TILE)
-            nc.vector.tensor_copy(
-                out=w_grouped[:, cols, :], in_=w_raw[:, :, cols].rearrange("p t n -> p n t")
-            )
-
-        def quantise_weights():
+        def prepare_weights():
+            for c in range(HID // N_TILE):
+                cols = slice(c * N_TILE, (c + 1) * N_TILE)
+                nc.vector.tensor_copy(
+                    out=w_grouped[:, cols, :], in_=w_raw[:, :, cols].rearrange("p t n -> p n t")
+                )
             nc.vector.quantize_mx(
                 out=w_codes[:].bitcast(FP8X4),
                 scales=w_scales[:],
                 in_=w_grouped[:].rearrange("p n t -> p (n t)"),
             )
 
-        def folds(b, which):
-            if b in FOLDED:
-                fold(b, which, 0)
-                fold(b, which, HALF // 2)
-
-        for m in range(BATCH + 2):
+        for m in range(BATCH + 3):
             counting = m < BATCH
-            dividing = 1 <= m <= BATCH
-            finishing = m >= 2
-            if finishing:
-                quantise_and_multiply(m - 2)
-            if dividing:
-                turn_sums(m - 1)
+            summing = 1 <= m <= BATCH
+            turning = 2 <= m <= BATCH + 1
+            finishing = m >= 3
             if counting:
-                count_rows(m, 0, SCALAR_ROWS)
+                count_rows(m, 0, 1)
+            if finishing:
+                turn_hidden(m - 3)
+                group_hidden(m - 3)
+            if counting:
                 merge_rows(m)
-                folds(m, 1)
-            if dividing:
+            if finishing:
+                quantise(m - 3)
+            if summing:
+                sum_slots(m - 1, 1)
                 count_matmul(m - 1)
             if finishing:
-                add_bias(m - 2, 0)
-            if dividing:
+                multiply(m - 3)
+            if counting:
+                fold(m, 1, 0)
+                count_rows(m, 1, 4)
+            if turning:
+                copy_sums(m - 2)
+                turn_sums(m - 2)
+            if summing:
+                sum_slots(m - 1, 0)
                 clamp_count(m - 1)
-            if finishing:
-                add_bias(m - 2, 1)
-            if dividing:
-                invert_count(m - 1)
-            if finishing:
-                leaky_and_store(m - 2, 0)
-            if dividing:
-                copy_inverse(m - 1)
             if counting:
                 reduce_rows(m)
-                sign_rows(m)
-                folds(m, 0)
-                sum_slots(m)
-            if dividing:
-                divide(m - 1)
-                group_hidden(m - 1)
-            if m == 1:
-                prepare_weights(0)
-                prepare_weights(1)
-                quantise_weights()
+                count_rows(m, 4, 8)
             if finishing:
-                leaky_and_store(m - 2, 1)
+                add_bias(m - 3, 0)
+            if summing:
+                invert_count(m - 1)
+            if turning:
+                divide(m - 2)
+            if counting:
+                fold(m, 1, 1)
+            if finishing:
+                add_bias(m - 3, 1)
+            if counting:
+                count_rows(m, 8, SLOTS)
+                sign_rows(m)
+                fold(m, 0, 0)
+            if finishing:
+                leaky_and_store(m - 3, 0)
+            if counting:
+                fold(m, 0, 1)
+            if m == 1:
+                prepare_weights()
+            if finishing:
+                leaky_and_store(m - 3, 1)

@@ -18,14 +18,16 @@ PACK = 4
 BATCH, NODES, SLOTS, FEAT, HID = 8, 128, 16, 256, 1024
 K = 2 * FEAT
 CHUNKS = K // P
-GROUP_NODES = P // SLOTS
+RUN = 2
+RUNS = SLOTS // RUN
+GROUP_NODES = P // RUNS
 GROUPS = NODES // GROUP_NODES
 HALF = SLOTS // 2
 N_TILE = 512
 SLOPE = 0.01
 BITS = 0x7FFF7FFF
-FOLDED = (0, 1)
-VECTOR_ROWS = 6
+FOLDED_SRC = (0, 1)
+VECTOR_ROWS = 4
 
 FLOPS = 2 * BATCH * NODES * K * HID
 
@@ -41,8 +43,7 @@ def tile_syntacticgcn_kernel(tc, src, neigh, w_map, b_map, out):
         psum_sums = ctx.enter_context(tc.psum_pool(name="psum_sums", bufs=2))
         psum_turned = ctx.enter_context(tc.psum_pool(name="psum_turned", bufs=1))
         psum_hidden = ctx.enter_context(tc.psum_pool(name="psum_hidden", bufs=1))
-        psum_num = ctx.enter_context(tc.psum_pool(name="psum_num", bufs=1))
-        psum_out = ctx.enter_context(tc.psum_pool(name="psum_out", bufs=3))
+        psum_out = ctx.enter_context(tc.psum_pool(name="psum_out", bufs=4))
         ctx.enter_context(tc.manual_schedule())
 
         raw = {}
@@ -50,7 +51,6 @@ def tile_syntacticgcn_kernel(tc, src, neigh, w_map, b_map, out):
         abs_sums = {}
         abs_values = {}
         merged = {}
-        valids = {}
         counts = {}
         inverses = {}
         sum_banks = {}
@@ -65,18 +65,21 @@ def tile_syntacticgcn_kernel(tc, src, neigh, w_map, b_map, out):
 
         def load(b, which):
             x = (src, neigh)[which]
-            t = loads.tile([P, SLOTS, FEAT], BF16, name="raw%d" % which)
-            raw[(b, which)] = t
-            if b in FOLDED:
+            if which == 1 or b in FOLDED_SRC:
+                t = loads.tile([P, SLOTS, FEAT], BF16, name="raw%d" % which)
                 rows = x[b]
+                count = SLOTS
             else:
-                rows = x[b].rearrange("(g j) s f -> (j s) g f", j=GROUP_NODES)
-            for first in range(0, SLOTS, HALF):
-                half = slice(first, first + HALF)
+                t = loads.tile([P, GROUPS, RUN * FEAT], BF16, name="raw%d" % which)
+                rows = x[b].rearrange("(g j) (q i) f -> (j q) g (i f)", j=GROUP_NODES, i=RUN)
+                count = GROUPS
+            raw[(b, which)] = t
+            for first in range(0, count, count // 2):
+                half = slice(first, first + count // 2)
                 nc.sync.dma_start(out=t[:, half, :], in_=rows[:, half, :])
 
         def vector_rows(b):
-            return 0 if b in FOLDED else VECTOR_ROWS
+            return 0 if b in FOLDED_SRC else VECTOR_ROWS
 
         def count_rows(b, first, last):
             if first == 0:
@@ -124,38 +127,11 @@ def tile_syntacticgcn_kernel(tc, src, neigh, w_map, b_map, out):
             )
 
         def sign_rows(b):
-            if b in FOLDED:
-                valid = work.tile([P, SLOTS], F32)
-                num = work.tile([P, 1], F32)
-                nc.scalar.activation(out=valid[:], in_=abs_sums[b][:], func=ACT.Sign, accum_out=num[:])
-                counts[b] = num
-            else:
-                valid_bf = work.tile([P, GROUPS], BF16)
-                nc.scalar.activation(out=valid_bf[:], in_=abs_sums[b][:], func=ACT.Sign)
-                own_valid = work.tile([P, GROUPS, GROUP_NODES], BF16)
-                nc.gpsimd.tensor_tensor(
-                    out=own_valid[:],
-                    in0=valid_bf[:].unsqueeze(2).to_broadcast([P, GROUPS, GROUP_NODES]),
-                    in1=select[:].unsqueeze(1).to_broadcast([P, GROUPS, GROUP_NODES]),
-                    op=ALU.mult,
-                )
-                valids[b] = own_valid
-
-        def count_matmul(b):
-            if b not in FOLDED:
-                num_t = psum_num.tile([P, 1], F32)
-                nc.tensor.matmul(
-                    out=num_t[:],
-                    lhsT=valids[b][:].rearrange("p g j -> p (g j)"),
-                    rhs=ones[:],
-                    start=True,
-                    stop=True,
-                )
-                counts[b] = num_t
-
-        def clamp_count(b):
+            valid = work.tile([P, SLOTS], F32)
+            num = work.tile([P, 1], F32)
+            nc.scalar.activation(out=valid[:], in_=abs_sums[b][:], func=ACT.Sign, accum_out=num[:])
             num_floor = work.tile([P, 1], F32)
-            nc.vector.tensor_scalar_max(out=num_floor[:], in0=counts[b][:], scalar1=1.0)
+            nc.gpsimd.tensor_scalar_max(out=num_floor[:], in0=num[:], scalar1=1.0)
             counts[b] = num_floor
 
         def invert_count(b):
@@ -164,10 +140,10 @@ def tile_syntacticgcn_kernel(tc, src, neigh, w_map, b_map, out):
             inverses[b] = inv_num
 
         def fold(b, which, part):
-            if b not in FOLDED:
+            if which == 0 and b not in FOLDED_SRC:
                 return
             if part == 0:
-                pair_sums = scratch.tile([P, HALF, FEAT], F32, name="pairs%d" % which)
+                pair_sums = work.tile([P, HALF, FEAT], F32, name="pairs%d" % which)
                 folded[(b, which)] = pair_sums
             quarter = HALF // 2
             first = part * HALF
@@ -183,7 +159,7 @@ def tile_syntacticgcn_kernel(tc, src, neigh, w_map, b_map, out):
                 sums_t = psum_sums.tile([P, CHUNKS, NODES], F32)
                 sum_banks[b] = sums_t
             chunks = range(which * CHUNKS // 2, (which + 1) * CHUNKS // 2)
-            if b in FOLDED:
+            if (b, which) in folded:
                 for c in chunks:
                     first = c * P - which * FEAT
                     for s in range(HALF):
@@ -198,13 +174,15 @@ def tile_syntacticgcn_kernel(tc, src, neigh, w_map, b_map, out):
             else:
                 for g in range(GROUPS):
                     for c in chunks:
-                        nc.tensor.matmul(
-                            out=sum_banks[b][:, c, g * GROUP_NODES : (g + 1) * GROUP_NODES],
-                            lhsT=raw[(b, which)][:, g, c * P - which * FEAT : (c + 1) * P - which * FEAT],
-                            rhs=select[:],
-                            start=True,
-                            stop=True,
-                        )
+                        for i in range(RUN):
+                            first = i * FEAT + c * P
+                            nc.tensor.matmul(
+                                out=sum_banks[b][:, c, g * GROUP_NODES : (g + 1) * GROUP_NODES],
+                                lhsT=raw[(b, which)][:, g, first : first + P],
+                                rhs=select[:],
+                                start=(i == 0),
+                                stop=(i == RUN - 1),
+                            )
 
         def copy_sums(b):
             sums = work.tile([P, CHUNKS, NODES], F32)
@@ -282,19 +260,26 @@ def tile_syntacticgcn_kernel(tc, src, neigh, w_map, b_map, out):
             nc.vector.scalar_tensor_tensor(
                 out=v, in0=v, scalar=SLOPE, in1=v, op0=ALU.mult, op1=ALU.max
             )
-            nc.sync.dma_start(out=out[b * NODES : (b + 1) * NODES, cols], in_=v)
+            if b == BATCH - 1:
+                nc.sync.dma_start(out=out[b * NODES : (b + 1) * NODES, cols], in_=v)
+            elif c == HID // N_TILE - 1:
+                nc.sync.dma_start(out=out[b * NODES : (b + 1) * NODES, :], in_=result_tiles[b][:])
 
         w_raw = const.tile([P, PACK, HID], BF16)
         bias = const.tile([P, HID], BF16)
+        bias_rows = const.tile([P, P], BF16)
+        nc.vector.memset(bias_rows[:], 0.0)
         load(0, 1)
         load(0, 0)
+        nc.sync.dma_start(
+            out=bias_rows[0 : HID // P, :], in_=b_map.rearrange("(c p) -> c p", p=P)
+        )
         load(1, 1)
         load(1, 0)
         nc.sync.dma_start(out=w_raw[:], in_=w_map.rearrange("(p t) n -> p t n", t=PACK))
         load(2, 1)
         load(3, 1)
         load(2, 0)
-        nc.sync.dma_start(out=bias[:], in_=b_map.partition_broadcast(P))
         for b in range(3, BATCH):
             if b + 1 < BATCH:
                 load(b + 1, 1)
@@ -302,12 +287,12 @@ def tile_syntacticgcn_kernel(tc, src, neigh, w_map, b_map, out):
 
         identity = const.tile([P, P], F32)
         make_identity(nc, identity[:])
-        ones = const.tile([P, 1], BF16)
-        nc.gpsimd.memset(ones[:], 1.0)
+        identity_bf = const.tile([P, P], BF16)
+        nc.vector.tensor_copy(out=identity_bf[:], in_=identity[:])
         select_f32 = const.tile([P, GROUP_NODES], F32)
         nc.vector.tensor_reduce(
             out=select_f32[:],
-            in_=identity[:].rearrange("p (j s) -> p j s", s=SLOTS),
+            in_=identity[:].rearrange("p (j q) -> p j q", q=RUNS),
             axis=AXIS.X,
             op=ALU.add,
         )
@@ -316,6 +301,20 @@ def tile_syntacticgcn_kernel(tc, src, neigh, w_map, b_map, out):
         w_grouped = const.tile([P, HID, PACK], BF16, align_bytes=64)
         w_codes = const.tile([P, HID], U32, align_bytes=64)
         w_scales = const.tile([P, HID], U8, align_bytes=64)
+
+        def spread_bias():
+            cols_t = psum_out.tile([P, P], BF16, name="acc")
+            nc.tensor.transpose(cols_t[:], bias_rows[:], identity_bf[:])
+            bias_cols = const.tile([P, HID // P], BF16)
+            nc.scalar.copy(out=bias_cols[:], in_=cols_t[:, 0 : HID // P])
+            spread_t = psum_out.tile([P, HID], BF16, name="acc")
+            for c in range(HID // P):
+                nc.tensor.transpose(
+                    spread_t[:, c * P : (c + 1) * P],
+                    bias_cols[:, c : c + 1].to_broadcast([P, P]),
+                    identity_bf[:],
+                )
+            nc.scalar.copy(out=bias[:], in_=spread_t[:])
 
         def prepare_weights():
             for c in range(HID // N_TILE):
@@ -345,7 +344,6 @@ def tile_syntacticgcn_kernel(tc, src, neigh, w_map, b_map, out):
                 quantise(m - 3)
             if summing:
                 sum_slots(m - 1, 1)
-                count_matmul(m - 1)
             if finishing:
                 multiply(m - 3)
             if counting:
@@ -356,7 +354,6 @@ def tile_syntacticgcn_kernel(tc, src, neigh, w_map, b_map, out):
                 turn_sums(m - 2)
             if summing:
                 sum_slots(m - 1, 0)
-                clamp_count(m - 1)
             if counting:
                 reduce_rows(m)
                 count_rows(m, 4, 8)
@@ -379,6 +376,7 @@ def tile_syntacticgcn_kernel(tc, src, neigh, w_map, b_map, out):
             if counting:
                 fold(m, 0, 1)
             if m == 1:
+                spread_bias()
                 prepare_weights()
             if finishing:
                 leaky_and_store(m - 3, 1)

@@ -18,15 +18,11 @@ PACK = 4
 BATCH, NODES, SLOTS, FEAT, HID = 8, 128, 16, 256, 1024
 K = 2 * FEAT
 CHUNKS = K // P
-RUN = 2
-RUNS = SLOTS // RUN
-GROUP_NODES = P // RUNS
-GROUPS = NODES // GROUP_NODES
+RUNS = (2, 2, 2, 2, 1, 1, 1, 1)
 HALF = SLOTS // 2
 N_TILE = 512
 SLOPE = 0.01
 BITS = 0x7FFF7FFF
-FOLDED_SRC = (0, 1)
 VECTOR_ROWS = 4
 
 FLOPS = 2 * BATCH * NODES * K * HID
@@ -46,7 +42,8 @@ def tile_syntacticgcn_kernel(tc, src, neigh, w_map, b_map, out):
         psum_out = ctx.enter_context(tc.psum_pool(name="psum_out", bufs=4))
         ctx.enter_context(tc.manual_schedule())
 
-        raw = {}
+        neigh_tiles = {}
+        src_tiles = {}
         folded = {}
         abs_sums = {}
         abs_values = {}
@@ -63,46 +60,45 @@ def tile_syntacticgcn_kernel(tc, src, neigh, w_map, b_map, out):
         acc_banks = {}
         result_tiles = {}
 
-        def load(b, which):
-            x = (src, neigh)[which]
-            if which == 1 or b in FOLDED_SRC:
-                t = loads.tile([P, SLOTS, FEAT], BF16, name="raw%d" % which)
-                rows = x[b]
-                count = SLOTS
-            else:
-                t = loads.tile([P, GROUPS, RUN * FEAT], BF16, name="raw%d" % which)
-                rows = x[b].rearrange("(g j) (q i) f -> (j q) g (i f)", j=GROUP_NODES, i=RUN)
-                count = GROUPS
-            raw[(b, which)] = t
-            for first in range(0, count, count // 2):
-                half = slice(first, first + count // 2)
-                nc.sync.dma_start(out=t[:, half, :], in_=rows[:, half, :])
+        def load_neigh(b):
+            neigh_t = loads.tile([P, SLOTS, FEAT], BF16)
+            neigh_tiles[b] = neigh_t
+            for first in range(0, SLOTS, HALF):
+                half = slice(first, first + HALF)
+                nc.sync.dma_start(out=neigh_t[:, half, :], in_=neigh[b][:, half, :])
 
-        def vector_rows(b):
-            return 0 if b in FOLDED_SRC else VECTOR_ROWS
+        def group_nodes(b):
+            return P // (SLOTS // RUNS[b])
+
+        def load_src(b):
+            run, nodes = RUNS[b], group_nodes(b)
+            src_t = loads.tile([P, NODES // nodes, run * FEAT], BF16)
+            src_tiles[b] = src_t
+            by_group = src[b].rearrange("(g j) (q i) f -> (j q) g (i f)", j=nodes, i=run)
+            half_groups = NODES // nodes // 2
+            for first in (0, half_groups):
+                half = slice(first, first + half_groups)
+                nc.sync.dma_start(out=src_t[:, half, :], in_=by_group[:, half, :])
 
         def count_rows(b, first, last):
-            if first == 0:
+            if first == VECTOR_ROWS:
                 abs_sum = work.tile([P, SLOTS], F32)
                 abs_sums[b] = abs_sum
                 abs_tile = scratch.tile([P, SLOTS, FEAT], BF16)
                 abs_values[b] = abs_tile
-            for r in range(first, min(last, SLOTS - vector_rows(b))):
+            for r in range(first, last):
                 nc.scalar.activation(
                     out=abs_values[b][:, r, :],
-                    in_=raw[(b, 1)][:, r, :],
+                    in_=neigh_tiles[b][:, r, :],
                     func=ACT.Abs,
                     accum_out=abs_sums[b][:, r : r + 1],
                 )
 
         def merge_rows(b):
-            rows = vector_rows(b)
-            if rows == 0:
-                return
-            words = raw[(b, 1)][:].bitcast(I32)[:, SLOTS - rows : SLOTS, :]
+            words = neigh_tiles[b][:].bitcast(I32)[:, 0:VECTOR_ROWS, :]
             width = FEAT // 4
-            half = scratch.tile([P, rows, width], I32)
-            quarter = work.tile([P, rows, width // 2], I32)
+            half = scratch.tile([P, VECTOR_ROWS, width], I32)
+            quarter = work.tile([P, VECTOR_ROWS, width // 2], I32)
             nc.vector.tensor_tensor(
                 out=half[:], in0=words[:, :, 0:width], in1=words[:, :, width : 2 * width], op=ALU.bitwise_or
             )
@@ -115,15 +111,12 @@ def tile_syntacticgcn_kernel(tc, src, neigh, w_map, b_map, out):
             merged[b] = quarter
 
         def reduce_rows(b):
-            rows = vector_rows(b)
-            if rows == 0:
-                return
-            unsigned = work.tile([P, rows, FEAT // 8], I32)
+            unsigned = work.tile([P, VECTOR_ROWS, FEAT // 8], I32)
             nc.vector.tensor_scalar(
                 out=unsigned[:], in0=merged[b][:], scalar1=BITS, scalar2=None, op0=ALU.bitwise_and
             )
             nc.vector.tensor_reduce(
-                out=abs_sums[b][:, SLOTS - rows : SLOTS], in_=unsigned[:], axis=AXIS.X, op=ALU.max
+                out=abs_sums[b][:, 0:VECTOR_ROWS], in_=unsigned[:], axis=AXIS.X, op=ALU.max
             )
 
         def sign_rows(b):
@@ -139,50 +132,46 @@ def tile_syntacticgcn_kernel(tc, src, neigh, w_map, b_map, out):
             nc.vector.reciprocal(out=inv_num[:], in_=counts[b][:])
             inverses[b] = inv_num
 
-        def fold(b, which, part):
-            if which == 0 and b not in FOLDED_SRC:
-                return
+        def fold(b, part):
             if part == 0:
-                pair_sums = work.tile([P, HALF, FEAT], F32, name="pairs%d" % which)
-                folded[(b, which)] = pair_sums
+                pair_sums = work.tile([P, HALF, FEAT], F32)
+                folded[b] = pair_sums
             quarter = HALF // 2
             first = part * HALF
             nc.vector.tensor_tensor(
-                out=folded[(b, which)][:, part * quarter : (part + 1) * quarter, :],
-                in0=raw[(b, which)][:, first : first + quarter, :],
-                in1=raw[(b, which)][:, first + quarter : first + HALF, :],
+                out=folded[b][:, part * quarter : (part + 1) * quarter, :],
+                in0=neigh_tiles[b][:, first : first + quarter, :],
+                in1=neigh_tiles[b][:, first + quarter : first + HALF, :],
                 op=ALU.add,
             )
 
-        def sum_slots(b, which):
-            if b not in sum_banks:
-                sums_t = psum_sums.tile([P, CHUNKS, NODES], F32)
-                sum_banks[b] = sums_t
-            chunks = range(which * CHUNKS // 2, (which + 1) * CHUNKS // 2)
-            if (b, which) in folded:
-                for c in chunks:
-                    first = c * P - which * FEAT
-                    for s in range(HALF):
+        def sum_neigh(b):
+            sums_t = psum_sums.tile([P, CHUNKS, NODES], F32)
+            sum_banks[b] = sums_t
+            for c in range(FEAT // P):
+                for s in range(HALF):
+                    nc.tensor.matmul(
+                        out=sums_t[:, FEAT // P + c, :],
+                        lhsT=folded[b][:, s, c * P : (c + 1) * P],
+                        rhs=identity[:],
+                        is_transpose=True,
+                        start=(s == 0),
+                        stop=(s == HALF - 1),
+                    )
+
+        def sum_src(b):
+            run, nodes = RUNS[b], group_nodes(b)
+            for g in range(NODES // nodes):
+                for c in range(FEAT // P):
+                    for i in range(run):
+                        first = i * FEAT + c * P
                         nc.tensor.matmul(
-                            out=sum_banks[b][:, c, :],
-                            lhsT=folded[(b, which)][:, s, first : first + P],
-                            rhs=identity[:],
-                            is_transpose=True,
-                            start=(s == 0),
-                            stop=(s == HALF - 1),
+                            out=sum_banks[b][:, c, g * nodes : (g + 1) * nodes],
+                            lhsT=src_tiles[b][:, g, first : first + P],
+                            rhs=selects[run][:],
+                            start=(i == 0),
+                            stop=(i == run - 1),
                         )
-            else:
-                for g in range(GROUPS):
-                    for c in chunks:
-                        for i in range(RUN):
-                            first = i * FEAT + c * P
-                            nc.tensor.matmul(
-                                out=sum_banks[b][:, c, g * GROUP_NODES : (g + 1) * GROUP_NODES],
-                                lhsT=raw[(b, which)][:, g, first : first + P],
-                                rhs=select[:],
-                                start=(i == 0),
-                                stop=(i == RUN - 1),
-                            )
 
         def copy_sums(b):
             sums = work.tile([P, CHUNKS, NODES], F32)
@@ -268,45 +257,47 @@ def tile_syntacticgcn_kernel(tc, src, neigh, w_map, b_map, out):
         w_raw = const.tile([P, PACK, HID], BF16)
         bias = const.tile([P, HID], BF16)
         bias_rows = const.tile([P, P], BF16)
+        bias_cols = const.tile([P, HID // P], BF16)
         nc.vector.memset(bias_rows[:], 0.0)
-        load(0, 1)
-        load(0, 0)
+        load_neigh(0)
         nc.sync.dma_start(
             out=bias_rows[0 : HID // P, :], in_=b_map.rearrange("(c p) -> c p", p=P)
         )
-        load(1, 1)
-        load(1, 0)
+        load_neigh(1)
         nc.sync.dma_start(out=w_raw[:], in_=w_map.rearrange("(p t) n -> p t n", t=PACK))
-        load(2, 1)
-        load(3, 1)
-        load(2, 0)
-        for b in range(3, BATCH):
+        load_src(0)
+        for b in range(1, BATCH):
             if b + 1 < BATCH:
-                load(b + 1, 1)
-            load(b, 0)
+                load_neigh(b + 1)
+            load_src(b)
 
         identity = const.tile([P, P], F32)
         make_identity(nc, identity[:])
         identity_bf = const.tile([P, P], BF16)
         nc.vector.tensor_copy(out=identity_bf[:], in_=identity[:])
-        select_f32 = const.tile([P, GROUP_NODES], F32)
-        nc.vector.tensor_reduce(
-            out=select_f32[:],
-            in_=identity[:].rearrange("p (j q) -> p j q", q=RUNS),
-            axis=AXIS.X,
-            op=ALU.add,
-        )
-        select = const.tile([P, GROUP_NODES], BF16)
-        nc.vector.tensor_copy(out=select[:], in_=select_f32[:])
+        selects = {}
+        for run in (1, 2):
+            nodes = P // (SLOTS // run)
+            select_f32 = const.tile([P, nodes], F32, name="select_f32_%d" % run)
+            select = const.tile([P, nodes], BF16, name="select_%d" % run)
+            nc.vector.tensor_reduce(
+                out=select_f32[:],
+                in_=identity[:].rearrange("p (j q) -> p j q", j=nodes),
+                axis=AXIS.X,
+                op=ALU.add,
+            )
+            nc.vector.tensor_copy(out=select[:], in_=select_f32[:])
+            selects[run] = select
         w_grouped = const.tile([P, HID, PACK], BF16, align_bytes=64)
         w_codes = const.tile([P, HID], U32, align_bytes=64)
         w_scales = const.tile([P, HID], U8, align_bytes=64)
 
-        def spread_bias():
+        def turn_bias():
             cols_t = psum_out.tile([P, P], BF16, name="acc")
             nc.tensor.transpose(cols_t[:], bias_rows[:], identity_bf[:])
-            bias_cols = const.tile([P, HID // P], BF16)
             nc.scalar.copy(out=bias_cols[:], in_=cols_t[:, 0 : HID // P])
+
+        def spread_bias():
             spread_t = psum_out.tile([P, HID], BF16, name="acc")
             for c in range(HID // P):
                 nc.tensor.transpose(
@@ -320,7 +311,8 @@ def tile_syntacticgcn_kernel(tc, src, neigh, w_map, b_map, out):
             for c in range(HID // N_TILE):
                 cols = slice(c * N_TILE, (c + 1) * N_TILE)
                 nc.vector.tensor_copy(
-                    out=w_grouped[:, cols, :], in_=w_raw[:, :, cols].rearrange("p t n -> p n t")
+                    out=w_grouped[:, cols, :].rearrange("p (n i) t -> p n t i", i=PACK),
+                    in_=w_raw[:, :, cols].rearrange("p t (n i) -> p n t i", i=PACK),
                 )
             nc.vector.quantize_mx(
                 out=w_codes[:].bitcast(FP8X4),
@@ -334,7 +326,7 @@ def tile_syntacticgcn_kernel(tc, src, neigh, w_map, b_map, out):
             turning = 2 <= m <= BATCH + 1
             finishing = m >= 3
             if counting:
-                count_rows(m, 0, 1)
+                count_rows(m, 4, 5)
             if finishing:
                 turn_hidden(m - 3)
                 group_hidden(m - 3)
@@ -343,20 +335,22 @@ def tile_syntacticgcn_kernel(tc, src, neigh, w_map, b_map, out):
             if finishing:
                 quantise(m - 3)
             if summing:
-                sum_slots(m - 1, 1)
+                sum_neigh(m - 1)
             if finishing:
                 multiply(m - 3)
             if counting:
-                fold(m, 1, 0)
-                count_rows(m, 1, 4)
+                fold(m, 0)
+                count_rows(m, 5, 8)
             if turning:
                 copy_sums(m - 2)
                 turn_sums(m - 2)
             if summing:
-                sum_slots(m - 1, 0)
+                sum_src(m - 1)
             if counting:
                 reduce_rows(m)
-                count_rows(m, 4, 8)
+                count_rows(m, 8, 12)
+            if m == 0:
+                turn_bias()
             if finishing:
                 add_bias(m - 3, 0)
             if summing:
@@ -364,19 +358,18 @@ def tile_syntacticgcn_kernel(tc, src, neigh, w_map, b_map, out):
             if turning:
                 divide(m - 2)
             if counting:
-                fold(m, 1, 1)
+                fold(m, 1)
             if finishing:
                 add_bias(m - 3, 1)
             if counting:
-                count_rows(m, 8, SLOTS)
+                count_rows(m, 12, SLOTS)
+            if m == 0:
+                spread_bias()
+            if counting:
                 sign_rows(m)
-                fold(m, 0, 0)
             if finishing:
                 leaky_and_store(m - 3, 0)
-            if counting:
-                fold(m, 0, 1)
             if m == 1:
-                spread_bias()
                 prepare_weights()
             if finishing:
                 leaky_and_store(m - 3, 1)

@@ -320,56 +320,56 @@ def tile_syntacticgcn_kernel(tc, src, neigh, w_map, b_map, out):
                 in_=w_grouped[:].rearrange("p n t -> p (n t)"),
             )
 
-        for m in range(BATCH + 3):
+        fold(0, 0)
+        for m in range(BATCH + 4):
             counting = m < BATCH
             summing = 1 <= m <= BATCH
             turning = 2 <= m <= BATCH + 1
-            finishing = m >= 3
-            if counting:
-                count_rows(m, 4, 5)
-            if finishing:
-                turn_hidden(m - 3)
-                group_hidden(m - 3)
-            if counting:
-                merge_rows(m)
-            if finishing:
-                quantise(m - 3)
+            multiplying = 3 <= m <= BATCH + 2
+            ending = m >= 4
             if summing:
                 sum_neigh(m - 1)
-            if finishing:
-                multiply(m - 3)
-            if counting:
-                fold(m, 0)
-                count_rows(m, 5, 8)
+            if multiplying:
+                group_hidden(m - 3)
+            if ending:
+                add_bias(m - 4, 1)
+            if multiplying:
+                quantise(m - 3)
             if turning:
-                copy_sums(m - 2)
                 turn_sums(m - 2)
+            if ending:
+                leaky_and_store(m - 4, 0)
+                leaky_and_store(m - 4, 1)
+            if counting:
+                merge_rows(m)
+                fold(m, 1)
+                count_rows(m, 4, 10)
+            if m == 0:
+                turn_bias()
+            if turning:
+                divide(m - 2)
             if summing:
                 sum_src(m - 1)
             if counting:
                 reduce_rows(m)
-                count_rows(m, 8, 12)
-            if m == 0:
-                turn_bias()
-            if finishing:
-                add_bias(m - 3, 0)
-            if summing:
-                invert_count(m - 1)
-            if turning:
-                divide(m - 2)
+            if multiplying:
+                multiply(m - 3)
             if counting:
-                fold(m, 1)
-            if finishing:
-                add_bias(m - 3, 1)
-            if counting:
-                count_rows(m, 12, SLOTS)
+                count_rows(m, 10, 14)
             if m == 0:
                 spread_bias()
-            if counting:
-                sign_rows(m)
-            if finishing:
-                leaky_and_store(m - 3, 0)
+            if summing:
+                invert_count(m - 1)
             if m == 1:
                 prepare_weights()
-            if finishing:
-                leaky_and_store(m - 3, 1)
+            if m + 1 < BATCH:
+                fold(m + 1, 0)
+            if multiplying:
+                add_bias(m - 3, 0)
+            if turning:
+                turn_hidden(m - 2)
+            if summing:
+                copy_sums(m - 1)
+            if counting:
+                count_rows(m, 14, SLOTS)
+                sign_rows(m)

from contextlib import ExitStack

import concourse.mybir as mybir
from concourse.masks import make_identity

F32 = mybir.dt.float32
BF16 = mybir.dt.bfloat16
U32 = mybir.dt.uint32
U8 = mybir.dt.uint8
I32 = mybir.dt.int32
FP8X4 = mybir.dt.float8_e4m3fn_x4
ALU = mybir.AluOpType
ACT = mybir.ActivationFunctionType
AXIS = mybir.AxisListType

P = 128
PACK = 4
BATCH, NODES, SLOTS, FEAT, HID = 8, 128, 16, 256, 1024
K = 2 * FEAT
CHUNKS = K // P
RUNS = (2, 2, 2, 2, 1, 1, 1, 1)
HALF = SLOTS // 2
N_TILE = 512
SLOPE = 0.01
BITS = 0x7FFF7FFF
VECTOR_ROWS = 4

FLOPS = 2 * BATCH * NODES * K * HID


def tile_syntacticgcn_kernel(tc, src, neigh, w_map, b_map, out):
    nc = tc.nc
    with ExitStack() as ctx:
        const = ctx.enter_context(tc.tile_pool(name="const", bufs=1))
        loads = ctx.enter_context(tc.tile_pool(name="loads", bufs=BATCH))
        results = ctx.enter_context(tc.tile_pool(name="results", bufs=BATCH))
        scratch = ctx.enter_context(tc.tile_pool(name="scratch", bufs=1))
        work = ctx.enter_context(tc.tile_pool(name="work", bufs=2))
        psum_sums = ctx.enter_context(tc.psum_pool(name="psum_sums", bufs=2))
        psum_turned = ctx.enter_context(tc.psum_pool(name="psum_turned", bufs=1))
        psum_hidden = ctx.enter_context(tc.psum_pool(name="psum_hidden", bufs=1))
        psum_out = ctx.enter_context(tc.psum_pool(name="psum_out", bufs=4))
        ctx.enter_context(tc.manual_schedule())

        neigh_tiles = {}
        src_tiles = {}
        folded = {}
        abs_sums = {}
        abs_values = {}
        merged = {}
        counts = {}
        inverses = {}
        sum_banks = {}
        sums_tiles = {}
        turned_banks = {}
        hidden_tiles = {}
        hidden_banks = {}
        grouped_tiles = {}
        code_tiles = {}
        acc_banks = {}
        result_tiles = {}

        def load_neigh(b):
            neigh_t = loads.tile([P, SLOTS, FEAT], BF16)
            neigh_tiles[b] = neigh_t
            for first in range(0, SLOTS, HALF):
                half = slice(first, first + HALF)
                nc.sync.dma_start(out=neigh_t[:, half, :], in_=neigh[b][:, half, :])

        def group_nodes(b):
            return P // (SLOTS // RUNS[b])

        def load_src(b):
            run, nodes = RUNS[b], group_nodes(b)
            src_t = loads.tile([P, NODES // nodes, run * FEAT], BF16)
            src_tiles[b] = src_t
            by_group = src[b].rearrange("(g j) (q i) f -> (j q) g (i f)", j=nodes, i=run)
            half_groups = NODES // nodes // 2
            for first in (0, half_groups):
                half = slice(first, first + half_groups)
                nc.sync.dma_start(out=src_t[:, half, :], in_=by_group[:, half, :])

        def count_rows(b, first, last):
            if first == VECTOR_ROWS:
                abs_sum = work.tile([P, SLOTS], F32)
                abs_sums[b] = abs_sum
                abs_tile = scratch.tile([P, SLOTS, FEAT], BF16)
                abs_values[b] = abs_tile
            for r in range(first, last):
                nc.scalar.activation(
                    out=abs_values[b][:, r, :],
                    in_=neigh_tiles[b][:, r, :],
                    func=ACT.Abs,
                    accum_out=abs_sums[b][:, r : r + 1],
                )

        def merge_rows(b):
            words = neigh_tiles[b][:].bitcast(I32)[:, 0:VECTOR_ROWS, :]
            width = FEAT // 4
            half = scratch.tile([P, VECTOR_ROWS, width], I32)
            quarter = work.tile([P, VECTOR_ROWS, width // 2], I32)
            nc.vector.tensor_tensor(
                out=half[:], in0=words[:, :, 0:width], in1=words[:, :, width : 2 * width], op=ALU.bitwise_or
            )
            nc.vector.tensor_tensor(
                out=quarter[:],
                in0=half[:, :, 0 : width // 2],
                in1=half[:, :, width // 2 : width],
                op=ALU.bitwise_or,
            )
            merged[b] = quarter

        def reduce_rows(b):
            unsigned = work.tile([P, VECTOR_ROWS, FEAT // 8], I32)
            nc.vector.tensor_scalar(
                out=unsigned[:], in0=merged[b][:], scalar1=BITS, scalar2=None, op0=ALU.bitwise_and
            )
            nc.vector.tensor_reduce(
                out=abs_sums[b][:, 0:VECTOR_ROWS], in_=unsigned[:], axis=AXIS.X, op=ALU.max
            )

        def sign_rows(b):
            valid = work.tile([P, SLOTS], F32)
            num = work.tile([P, 1], F32)
            nc.scalar.activation(out=valid[:], in_=abs_sums[b][:], func=ACT.Sign, accum_out=num[:])
            num_floor = work.tile([P, 1], F32)
            nc.gpsimd.tensor_scalar_max(out=num_floor[:], in0=num[:], scalar1=1.0)
            counts[b] = num_floor

        def invert_count(b):
            inv_num = work.tile([P, 1], F32)
            nc.vector.reciprocal(out=inv_num[:], in_=counts[b][:])
            inverses[b] = inv_num

        def fold(b, part):
            if part == 0:
                pair_sums = work.tile([P, HALF, FEAT], F32)
                folded[b] = pair_sums
            quarter = HALF // 2
            first = part * HALF
            nc.vector.tensor_tensor(
                out=folded[b][:, part * quarter : (part + 1) * quarter, :],
                in0=neigh_tiles[b][:, first : first + quarter, :],
                in1=neigh_tiles[b][:, first + quarter : first + HALF, :],
                op=ALU.add,
            )

        def sum_neigh(b):
            sums_t = psum_sums.tile([P, CHUNKS, NODES], F32)
            sum_banks[b] = sums_t
            for c in range(FEAT // P):
                for s in range(HALF):
                    nc.tensor.matmul(
                        out=sums_t[:, FEAT // P + c, :],
                        lhsT=folded[b][:, s, c * P : (c + 1) * P],
                        rhs=identity[:],
                        is_transpose=True,
                        start=(s == 0),
                        stop=(s == HALF - 1),
                    )

        def sum_src(b):
            run, nodes = RUNS[b], group_nodes(b)
            for g in range(NODES // nodes):
                for c in range(FEAT // P):
                    for i in range(run):
                        first = i * FEAT + c * P
                        nc.tensor.matmul(
                            out=sum_banks[b][:, c, g * nodes : (g + 1) * nodes],
                            lhsT=src_tiles[b][:, g, first : first + P],
                            rhs=selects[run][:],
                            start=(i == 0),
                            stop=(i == run - 1),
                        )

        def copy_sums(b):
            sums = work.tile([P, CHUNKS, NODES], F32)
            nc.scalar.copy(out=sums[:], in_=sum_banks[b][:])
            sums_tiles[b] = sums

        def turn_sums(b):
            turned = psum_turned.tile([P, K], F32)
            for c in range(CHUNKS):
                nc.tensor.transpose(turned[:, c * P : (c + 1) * P], sums_tiles[b][:, c, :], identity[:])
            turned_banks[b] = turned

        def divide(b):
            hidden = work.tile([P, K], BF16)
            nc.scalar.copy(out=hidden[:, 0:FEAT], in_=turned_banks[b][:, 0:FEAT])
            nc.scalar.activation(
                out=hidden[:, FEAT:K],
                in_=turned_banks[b][:, FEAT:K],
                func=ACT.Copy,
                scale=inverses[b][:, 0:1],
            )
            hidden_tiles[b] = hidden

        def turn_hidden(b):
            hidden_t = psum_hidden.tile([P, PACK // 2, NODES], F32)
            words = hidden_tiles[b][:].bitcast(F32)
            for u in range(PACK // 2):
                nc.tensor.transpose(hidden_t[:, u, :], words[:, u : K // 2 : PACK // 2], identity[:])
            hidden_banks[b] = hidden_t

        def group_hidden(b):
            grouped = work.tile([P, NODES * PACK], BF16, align_bytes=64)
            nc.scalar.copy(
                out=grouped[:].bitcast(F32).rearrange("p (n u) -> p n u", u=PACK // 2),
                in_=hidden_banks[b][:].rearrange("p u n -> p n u"),
            )
            grouped_tiles[b] = grouped

        def quantise(b):
            h_codes = work.tile([P, NODES], U32, align_bytes=64)
            h_scales = work.tile([P, NODES], U8, align_bytes=64)
            nc.vector.quantize_mx(
                out=h_codes[:].bitcast(FP8X4), scales=h_scales[:], in_=grouped_tiles[b][:]
            )
            code_tiles[b] = (h_codes, h_scales)

        def multiply(b):
            h_codes, h_scales = code_tiles[b]
            for c in range(HID // N_TILE):
                cols = slice(c * N_TILE, (c + 1) * N_TILE)
                acc = psum_out.tile([P, N_TILE], F32)
                nc.tensor.matmul_mx(
                    out=acc[:],
                    lhsT=h_codes[:].bitcast(FP8X4),
                    lhsT_scale=h_scales[:],
                    rhs=w_codes[:, cols].bitcast(FP8X4),
                    rhs_scale=w_scales[:, cols],
                    start=True,
                    stop=True,
                )
                acc_banks[(b, c)] = acc

        def add_bias(b, c):
            if c == 0:
                result = results.tile([P, HID], F32)
                result_tiles[b] = result
            cols = slice(c * N_TILE, (c + 1) * N_TILE)
            nc.vector.tensor_tensor(
                out=result_tiles[b][:, cols], in0=acc_banks[(b, c)][:], in1=bias[:, cols], op=ALU.add
            )

        def leaky_and_store(b, c):
            cols = slice(c * N_TILE, (c + 1) * N_TILE)
            v = result_tiles[b][:, cols]
            nc.vector.scalar_tensor_tensor(
                out=v, in0=v, scalar=SLOPE, in1=v, op0=ALU.mult, op1=ALU.max
            )
            if b == BATCH - 1:
                nc.sync.dma_start(out=out[b * NODES : (b + 1) * NODES, cols], in_=v)
            elif c == HID // N_TILE - 1:
                nc.sync.dma_start(out=out[b * NODES : (b + 1) * NODES, :], in_=result_tiles[b][:])

        w_raw = const.tile([P, PACK, HID], BF16)
        bias = const.tile([P, HID], BF16)
        bias_rows = const.tile([P, P], BF16)
        bias_cols = const.tile([P, HID // P], BF16)
        nc.vector.memset(bias_rows[:], 0.0)
        load_neigh(0)
        nc.sync.dma_start(
            out=bias_rows[0 : HID // P, :], in_=b_map.rearrange("(c p) -> c p", p=P)
        )
        load_neigh(1)
        nc.sync.dma_start(out=w_raw[:], in_=w_map.rearrange("(p t) n -> p t n", t=PACK))
        load_src(0)
        for b in range(1, BATCH):
            if b + 1 < BATCH:
                load_neigh(b + 1)
            load_src(b)

        identity = const.tile([P, P], F32)
        make_identity(nc, identity[:])
        identity_bf = const.tile([P, P], BF16)
        nc.vector.tensor_copy(out=identity_bf[:], in_=identity[:])
        selects = {}
        for run in (1, 2):
            nodes = P // (SLOTS // run)
            select_f32 = const.tile([P, nodes], F32, name="select_f32_%d" % run)
            select = const.tile([P, nodes], BF16, name="select_%d" % run)
            nc.vector.tensor_reduce(
                out=select_f32[:],
                in_=identity[:].rearrange("p (j q) -> p j q", j=nodes),
                axis=AXIS.X,
                op=ALU.add,
            )
            nc.vector.tensor_copy(out=select[:], in_=select_f32[:])
            selects[run] = select
        w_grouped = const.tile([P, HID, PACK], BF16, align_bytes=64)
        w_codes = const.tile([P, HID], U32, align_bytes=64)
        w_scales = const.tile([P, HID], U8, align_bytes=64)

        def turn_bias():
            cols_t = psum_out.tile([P, P], BF16, name="acc")
            nc.tensor.transpose(cols_t[:], bias_rows[:], identity_bf[:])
            nc.scalar.copy(out=bias_cols[:], in_=cols_t[:, 0 : HID // P])

        def spread_bias():
            spread_t = psum_out.tile([P, HID], BF16, name="acc")
            for c in range(HID // P):
                nc.tensor.transpose(
                    spread_t[:, c * P : (c + 1) * P],
                    bias_cols[:, c : c + 1].to_broadcast([P, P]),
                    identity_bf[:],
                )
            nc.scalar.copy(out=bias[:], in_=spread_t[:])

        def prepare_weights():
            for c in range(HID // N_TILE):
                cols = slice(c * N_TILE, (c + 1) * N_TILE)
                nc.vector.tensor_copy(
                    out=w_grouped[:, cols, :].rearrange("p (n i) t -> p n t i", i=PACK),
                    in_=w_raw[:, :, cols].rearrange("p t (n i) -> p n t i", i=PACK),
                )
            nc.vector.quantize_mx(
                out=w_codes[:].bitcast(FP8X4),
                scales=w_scales[:],
                in_=w_grouped[:].rearrange("p n t -> p (n t)"),
            )

        fold(0, 0)
        for m in range(BATCH + 4):
            counting = m < BATCH
            summing = 1 <= m <= BATCH
            turning = 2 <= m <= BATCH + 1
            multiplying = 3 <= m <= BATCH + 2
            ending = m >= 4
            if summing:
                sum_neigh(m - 1)
            if multiplying:
                group_hidden(m - 3)
            if ending:
                add_bias(m - 4, 1)
            if multiplying:
                quantise(m - 3)
            if turning:
                turn_sums(m - 2)
            if ending:
                leaky_and_store(m - 4, 0)
                leaky_and_store(m - 4, 1)
            if counting:
                merge_rows(m)
                fold(m, 1)
                count_rows(m, 4, 10)
            if m == 0:
                turn_bias()
            if turning:
                divide(m - 2)
            if summing:
                sum_src(m - 1)
            if counting:
                reduce_rows(m)
            if multiplying:
                multiply(m - 3)
            if counting:
                count_rows(m, 10, 14)
            if m == 0:
                spread_bias()
            if summing:
                invert_count(m - 1)
            if m == 1:
                prepare_weights()
            if m + 1 < BATCH:
                fold(m + 1, 0)
            if multiplying:
                add_bias(m - 3, 0)
            if turning:
                turn_hidden(m - 2)
            if summing:
                copy_sums(m - 1)
            if counting:
                count_rows(m, 14, SLOTS)
                sign_rows(m)
